import numpy as np
import ml_dtypes


def mxq(x, axis, fmt="e4m3"):
    dtype, down = {"e4m3": (ml_dtypes.float8_e4m3fn, 7), "e5m2": (ml_dtypes.float8_e5m2, 14)}[fmt]
    v = np.moveaxis(np.asarray(x, np.float32).astype(ml_dtypes.bfloat16).astype(np.float64), axis, -1)
    blocks = v.reshape(v.shape[:-1] + (-1, 32))
    amax = np.abs(blocks).max(-1, keepdims=True)
    byte = np.maximum(np.where(amax > 0, np.frexp(amax)[1] - 1 + 127, 0) - down, 1)
    scale = np.exp2(byte - 127.0)
    codes = (blocks / scale).astype(np.float32).astype(dtype).astype(np.float64)
    return np.moveaxis((codes * scale).reshape(v.shape), -1, axis)


WIDE = False


def mx_kscale(k):
    if not WIDE:
        return np.ones(k)
    levels = np.array([30, -30])
    if k % 512:
        return np.exp2(np.random.permutation(np.resize(levels, k // 32))).repeat(32)
    a = np.empty((k // 512, 16))
    for p in range(k // 512):
        a[p, :8] = np.random.permutation(np.resize(levels, 8))
        for g in range(8):
            far = levels[np.abs(levels - a[p, g]) >= 10]
            a[p, g + 8] = far[np.random.randint(len(far))]
    return np.exp2(a.ravel()).repeat(32)


BF16 = ml_dtypes.bfloat16


def bf(x):
    return np.asarray(x, np.float32).astype(BF16)


def f64(x):
    return np.asarray(x).astype(np.float64)


B, S, HIDDEN, H, KV, D, SEC_T, SEC_H, SEC_W, PAD = 1, 1024, 2048, 16, 2, 128, 16, 24, 24, 256
SECTIONS = (SEC_T, SEC_H, SEC_W)
VALID = S - PAD


def rotate_half(t):
    t1, t2 = np.split(t, 2, axis=-1)
    return np.concatenate((-t2, t1), axis=-1)


def reorder(t):
    chunks = []
    idx = 0
    for i in range(2 * len(SECTIONS)):
        sec = SECTIONS[i % len(SECTIONS)]
        chunks.append(t[i % len(SECTIONS), ..., idx:idx + sec])
        idx += sec
    return np.concatenate(chunks, axis=-1)


def setup_inputs():
    sc = mx_kscale(HIDDEN)
    w = 1.0 / np.sqrt(HIDDEN)
    ang = np.random.uniform(0.0, 2.0 * np.pi, (len(SECTIONS), B, S, D))
    mask = (np.arange(S)[None, :] < VALID) * np.ones((B, 1))
    return {"x": bf(np.random.standard_normal((B, S, HIDDEN)) * sc),
            "cos": bf(np.cos(ang)), "sin": bf(np.sin(ang)), "mask": bf(mask),
            "Wq": bf(np.random.standard_normal((HIDDEN, H * D)) * w / sc[:, None]), "bq": bf(np.random.standard_normal(H * D) * 0.2),
            "Wk": bf(np.random.standard_normal((HIDDEN, KV * D)) * w / sc[:, None]), "bk": bf(np.random.standard_normal(KV * D) * 0.2),
            "Wv": bf(np.random.standard_normal((HIDDEN, KV * D)) * w / sc[:, None]), "bv": bf(np.random.standard_normal(KV * D) * 0.2)}


def reference(x, cos, sin, mask, Wq, bq, Wk, bk, Wv, bv):
    xq = mxq(f64(x), 2, "e5m2")
    q = ((xq @ mxq(f64(Wq), 0, "e4m3")) + f64(bq)).reshape(B, S, H, D).transpose(0, 2, 1, 3)
    k = ((xq @ mxq(f64(Wk), 0, "e4m3")) + f64(bk)).reshape(B, S, KV, D).transpose(0, 2, 1, 3)
    v = ((xq @ mxq(f64(Wv), 0, "e4m3")) + f64(bv)).reshape(B, S, KV, D).transpose(0, 2, 1, 3)
    cos_e = reorder(f64(cos))[:, None]
    sin_e = reorder(f64(sin))[:, None]
    q = q * cos_e + rotate_half(q) * sin_e
    k = k * cos_e + rotate_half(k) * sin_e
    bm = f64(mask)[:, None, :, None]
    return q, k * bm, v * bm

@@ -1,0 +1,360 @@
+from contextlib import ExitStack
+
+import concourse.mybir as mybir
+from concourse.masks import make_identity
+
+S, HIDDEN, H, KV, D = 1024, 2048, 16, 2, 128
+SECTIONS = ((0, 16), (16, 40), (40, 64))
+
+FLOPS = 2 * S * HIDDEN * (H + 2 * KV) * D
+BYTES = 2 * (S * HIDDEN + 2 * S * D + S + (HIDDEN + 1) * (H + 2 * KV) * D) + 4 * S * (H + 2 * KV) * D
+
+F32 = mybir.dt.float32
+BF16 = mybir.dt.bfloat16
+U32 = mybir.dt.uint32
+U8 = mybir.dt.uint8
+E4M3 = mybir.dt.float8_e4m3fn_x4
+E5M2 = mybir.dt.float8_e5m2_x4
+MULT = mybir.AluOpType.mult
+ADD = mybir.AluOpType.add
+ACT = mybir.ActivationFunctionType
+
+P = 128
+PACK = 4
+K_PASS = P * PACK
+PASSES = HIDDEN // K_PASS
+TOK = S // P
+HALF_TOK = TOK // 2
+N_HALF = HALF_TOK * P
+PAIR = 2 * D
+HD = D // 2
+Q_PAIRS = H // 2
+NARROW_PAIRS = 4
+
+
+def tile_multiheadattention_pa_kernel(tc, x, cos, sin, mask, Wq, bq, Wk, bk, Wv, bv, out_0, out_1, out_2):
+    nc = tc.nc
+    x_tok = x[0].rearrange("(p j) k -> p j k", j=TOK)
+
+    with ExitStack() as ctx:
+        keep = ctx.enter_context(tc.tile_pool(name="keep", bufs=1))
+        ring = ctx.enter_context(tc.tile_pool(name="ring", bufs=1))
+        psum = ctx.enter_context(tc.psum_pool(name="psum", bufs=4))
+        ctx.enter_context(tc.manual_schedule())
+
+        ident = keep.tile([P, P], F32)
+        ident_bf = keep.tile([P, P], BF16)
+        bias_rows = keep.tile([P, D], BF16)
+        bias_cols = keep.tile([P, H + KV], F32)
+        bv_all = keep.tile([P, PAIR], F32)
+        bv_masked = keep.tile([P, TOK, PAIR], F32)
+        mask_bf = keep.tile([P, TOK], BF16)
+        mask_f32 = keep.tile([P, TOK], F32)
+        rot = keep.tile([P, TOK, 4, HD], BF16)
+        rot_last = keep.tile([P, 2 * TOK, 2, 32], BF16)
+        v_out = keep.tile([P, KV, TOK, D], F32)
+        x_codes = {}
+        x_scales = {}
+        for hh in range(2):
+            for g in range(PASSES):
+                x_codes[hh, g] = keep.tile([P, N_HALF], U32, align_bytes=64, name="x_codes_%d_%d" % (hh, g))
+                x_scales[hh, g] = keep.tile([P, N_HALF], U8, align_bytes=64, name="x_scales_%d_%d" % (hh, g))
+
+        x_raw, x_grouped = {}, {}
+        w_raw, w_grouped, w_codes, w_scales = {}, {}, {}, {}
+        acc, chan_major, tok_major, prod_a, prod_b = {}, {}, {}, {}, {}
+
+        def load_x(hh, g):
+            t = ring.tile([P, HALF_TOK, K_PASS], BF16, tag="raw_wide", bufs=8, name="x_raw")
+            nc.sync.dma_start(out=t[:], in_=x_tok[:, hh * HALF_TOK:(hh + 1) * HALF_TOK, g * K_PASS:(g + 1) * K_PASS])
+            x_raw[hh, g] = t
+
+        def load_w(pairs, W, col0, g):
+            width = PAIR * len(pairs)
+            if len(pairs) == 1:
+                t = ring.tile([P, PACK, width], BF16, tag="raw_narrow", bufs=16, name="w_narrow")
+            else:
+                t = ring.tile([P, PACK, width], BF16, tag="raw_wide", bufs=8, name="w_wide")
+            rows = W[g * K_PASS:(g + 1) * K_PASS, col0:col0 + width]
+            nc.sync.dma_start(out=t[:], in_=rows.rearrange("(p j) n -> p j n", j=PACK))
+            for i, pair in enumerate(pairs):
+                w_raw[pair, g] = t[:, :, i * PAIR:(i + 1) * PAIR]
+
+        def load_table(hh, cs, axis):
+            lo, hi = SECTIONS[axis]
+            rows = slice(hh * TOK, (hh + 1) * TOK)
+            src = (cos, sin)[cs][axis, 0].rearrange("(p j) (f d) -> p (j f) d", j=TOK, f=2)[:, rows, lo:hi]
+            if axis < 2:
+                dst = rot[:].rearrange("p j (f c) d -> p (j f) c d", c=2)[:, rows, cs, lo:hi]
+            else:
+                dst = rot_last[:, rows, cs, 0:hi - lo]
+            nc.sync.dma_start(out=dst, in_=src)
+
+        def finish_tables(hh):
+            lo, hi = SECTIONS[2]
+            rows = slice(hh * TOK, (hh + 1) * TOK)
+            nc.vector.tensor_copy(out=rot[:].rearrange("p j (f c) d -> p (j f) c d", c=2)[:, rows, :, lo:hi],
+                                  in_=rot_last[:, rows, :, 0:hi - lo])
+            first_sin = rot[:, hh * HALF_TOK:(hh + 1) * HALF_TOK, 1, :]
+            nc.vector.tensor_scalar(out=first_sin, in0=first_sin, scalar1=-1.0, scalar2=None, op0=MULT)
+
+        def transpose_x(hh, g):
+            words = x_raw[hh, g][:].rearrange("p j k -> p (j k)").bitcast(F32)
+            grouped = ring.tile([P, N_HALF * PACK], BF16, tag="x_grouped", bufs=3, align_bytes=64, name="x_grouped")
+            x_grouped[hh, g] = grouped
+            for b in range(2):
+                bank = psum.tile([P, 2, 2, P], F32, tag="turned", name="x_bank")
+                for jj in range(2):
+                    w0 = (2 * b + jj) * (K_PASS // 2)
+                    for u in range(2):
+                        nc.tensor.transpose(bank[:, jj, u, :], words[:, w0 + u:w0 + K_PASS // 2:2], ident[:])
+                dst = grouped[:, b * 2 * P * PACK:(b + 1) * 2 * P * PACK].bitcast(F32)
+                nc.scalar.copy(out=dst.rearrange("p (j r u) -> p j r u", j=2, u=2), in_=bank[:].rearrange("p j u r -> p j r u"))
+
+        def quantize_x(hh, g):
+            nc.vector.quantize_mx(out=x_codes[hh, g][:].bitcast(E5M2), scales=x_scales[hh, g][:], in_=x_grouped[hh, g][:])
+
+        def interleave_w(pair, g, on_vector):
+            if pair not in w_grouped:
+                w_grouped[pair] = ring.tile([P, PASSES, PAIR, PACK], BF16, tag="w_grouped", bufs=3, align_bytes=64, name="w_grouped")
+            dst = w_grouped[pair][:, g].rearrange("p (c i) t -> p c t i", i=4)
+            src = w_raw[pair, g].rearrange("p t (c i) -> p c t i", i=4)
+            if on_vector:
+                nc.vector.tensor_copy(out=dst, in_=src)
+            else:
+                nc.scalar.copy(out=dst, in_=src)
+
+        def quantize_w(pair, g0, g1):
+            if pair not in w_codes:
+                w_codes[pair] = ring.tile([P, PASSES, PAIR], U32, tag="w_codes", bufs=4, align_bytes=64, name="w_codes")
+                w_scales[pair] = ring.tile([P, PASSES, PAIR], U8, tag="w_scales", bufs=4, align_bytes=64, name="w_scales")
+            nc.vector.quantize_mx(out=w_codes[pair][:, g0:g1].rearrange("p g n -> p (g n)").bitcast(E4M3),
+                                  scales=w_scales[pair][:, g0:g1].rearrange("p g n -> p (g n)"),
+                                  in_=w_grouped[pair][:, g0:g1].rearrange("p g n t -> p (g n t)"))
+
+        def pair_of(head):
+            return ("k", head - H) if head >= H else (head // 2, head % 2)
+
+        def project(head, hh, g):
+            pair, i = pair_of(head)
+            if g == 0:
+                acc[head, hh] = psum.tile([P, N_HALF], F32, tag="acc", name="acc")
+            cols = slice(i * D, (i + 1) * D)
+            nc.tensor.matmul_mx(out=acc[head, hh][:], lhsT=w_codes[pair][:, g, cols].bitcast(E4M3), lhsT_scale=w_scales[pair][:, g, cols],
+                                rhs=x_codes[hh, g][:].bitcast(E5M2), rhs_scale=x_scales[hh, g][:],
+                                start=(g == 0), stop=(g == PASSES - 1))
+
+        def project_all(head, hh):
+            for g in range(PASSES):
+                project(head, hh, g)
+
+        def add_bias(head, hh):
+            t = ring.tile([P, N_HALF], F32, tag="chan_major", bufs=6, name="chan_major")
+            nc.scalar.activation(out=t[:], in_=acc[head, hh][:], func=ACT.Identity, bias=bias_cols[:, head:head + 1])
+            chan_major[head, hh] = t
+
+        def transpose_out(head, hh):
+            bank = psum.tile([P, HALF_TOK, D], F32, tag="turned", name="out_bank")
+            for j in range(HALF_TOK):
+                nc.tensor.transpose(bank[:, j, :], chan_major[head, hh][:, j * P:(j + 1) * P], ident[:])
+            tok_major[head, hh] = bank
+
+        def rotate(head, hh):
+            if hh == 0:
+                prod_a[head] = ring.tile([P, TOK, 2, HD], F32, tag="prod_a", bufs=6, name="prod_a")
+                prod_b[head] = ring.tile([P, TOK, 2, HD], F32, tag="prod_b", bufs=3, name="prod_b")
+            bank = tok_major[head, hh]
+            j0 = hh * HALF_TOK
+            for prod, f, slots in ((prod_a[head], 0, slice(0, 4, 3)), (prod_b[head], 1, slice(1, 3))):
+                feats = slice(f * HD, (f + 1) * HD)
+                if head < H:
+                    nc.vector.tensor_tensor(out=prod[:, j0:j0 + HALF_TOK],
+                                            in0=bank[:, :, feats].unsqueeze(2).to_broadcast([P, HALF_TOK, 2, HD]),
+                                            in1=rot[:, j0:j0 + HALF_TOK, slots, :], op=MULT)
+                else:
+                    for j in range(j0, j0 + HALF_TOK):
+                        nc.vector.scalar_tensor_tensor(out=prod[:, j], in0=bank[:, j - j0, feats].unsqueeze(1).to_broadcast([P, 2, HD]),
+                                                       scalar=mask_f32[:, j:j + 1], in1=rot[:, j, slots, :], op0=MULT, op1=MULT)
+
+        def add_products(head, j0, j1):
+            a = prod_a[head][:, j0:j1].rearrange("p j f d -> p (j f d)")
+            b = prod_b[head][:, j0:j1].rearrange("p j f d -> p (j f d)")
+            nc.gpsimd.tensor_tensor(out=a, in0=a, in1=b, op=ADD)
+
+        def store_head(head, j0, j1):
+            dst = out_1[0, head - H] if head >= H else out_0[0, head]
+            nc.sync.dma_start(out=dst.rearrange("(p j) d -> p j d", j=TOK)[:, j0:j1, :],
+                              in_=prod_a[head][:, j0:j1].rearrange("p j f d -> p j (f d)"))
+
+        def project_v(b):
+            bank = psum.tile([P, 2, PAIR], F32, tag="acc", name="v_acc")
+            acc["v", b] = bank
+            for jj in range(2):
+                hh, j = divmod(2 * b + jj, HALF_TOK)
+                toks = slice(j * P, (j + 1) * P)
+                for g in range(PASSES):
+                    nc.tensor.matmul_mx(out=bank[:, jj, :], lhsT=x_codes[hh, g][:, toks].bitcast(E5M2), lhsT_scale=x_scales[hh, g][:, toks],
+                                        rhs=w_codes["v"][:, g, :].bitcast(E4M3), rhs_scale=w_scales["v"][:, g, :],
+                                        start=(g == 0), stop=(g == PASSES - 1))
+
+        def finish_v(b):
+            for jj in range(2):
+                j = 2 * b + jj
+                nc.vector.scalar_tensor_tensor(out=v_out[:, :, j, :], in0=acc["v", b][:, jj, :].rearrange("p (h d) -> p h d", h=KV),
+                                               scalar=mask_f32[:, j:j + 1], in1=bv_masked[:, j, :].rearrange("p (h d) -> p h d", h=KV),
+                                               op0=MULT, op1=ADD)
+            nc.sync.dma_start(out=out_2[0].rearrange("h (p j) d -> p h j d", j=TOK)[:, :, 2 * b:2 * b + 2, :],
+                              in_=v_out[:, :, 2 * b:2 * b + 2, :])
+
+        make_identity(nc, ident[:])
+        make_identity(nc, ident_bf[:])
+        nc.vector.memset(bias_rows[:], 0.0)
+        for g in range(2):
+            load_x(0, g)
+            load_w(["k"], Wk, 0, g)
+        nc.scalar.dma_start(out=mask_bf[:], in_=mask[0].rearrange("(p j) -> p j", j=TOK))
+        nc.scalar.dma_start(out=bias_rows[0:H, :], in_=bq.rearrange("(h d) -> h d", d=D))
+        nc.scalar.dma_start(out=bias_rows[H:H + KV, :], in_=bk.rearrange("(h d) -> h d", d=D))
+        nc.scalar.dma_start(out=bias_rows[H + KV:H + 2 * KV, :], in_=bv.rearrange("(h d) -> h d", d=D))
+        nc.scalar.activation(out=mask_f32[:], in_=mask_bf[:], func=ACT.Identity)
+        for g in range(2, PASSES):
+            load_x(0, g)
+            load_w(["k"], Wk, 0, g)
+        tables = [(cs, axis) for axis in range(3) for cs in range(2)]
+        load_x(1, 0)
+        load_table(0, *tables[0])
+        load_w([0], Wq, 0, 0)
+        load_table(0, *tables[1])
+        load_x(1, 1)
+        load_table(0, *tables[2])
+        load_w([0], Wq, 0, 1)
+        load_table(0, *tables[3])
+        load_w([0], Wq, 0, 2)
+        load_table(0, *tables[4])
+        load_x(1, 2)
+        load_table(0, *tables[5])
+        load_w([0], Wq, 0, 3)
+        load_x(1, 3)
+        for g in range(PASSES):
+            load_w([1], Wq, PAIR, g)
+        for cs, axis in tables:
+            load_table(1, cs, axis)
+        for pair in range(2, NARROW_PAIRS):
+            for g in range(PASSES):
+                load_w([pair], Wq, pair * PAIR, g)
+        for g in range(PASSES):
+            load_w([4, 5], Wq, 4 * PAIR, g)
+
+        transpose_x(0, 0)
+        bias_bank = psum.tile([P, P], BF16, tag="acc", name="bias_bank")
+        nc.tensor.transpose(bias_bank[:], bias_rows[:], ident_bf[:])
+        bv_bank = psum.tile([P, PAIR], F32, tag="acc", name="bv_bank")
+        for i in range(KV):
+            row = H + KV + i
+            nc.tensor.matmul(bv_bank[:, i * D:(i + 1) * D], lhsT=ident_bf[:, row:row + 1].to_broadcast([P, P]), rhs=bias_rows[:],
+                             start=True, stop=True)
+        for g in range(PASSES):
+            if g + 1 < PASSES:
+                transpose_x(0, g + 1)
+            else:
+                transpose_x(1, 0)
+            interleave_w("k", g, True)
+            if g == 0:
+                nc.vector.tensor_copy(out=bias_cols[:], in_=bias_bank[:, 0:H + KV])
+                nc.vector.tensor_copy(out=bv_all[:], in_=bv_bank[:])
+            quantize_x(0, g)
+            quantize_w("k", g, g + 1)
+            for i in range(KV):
+                project(H + i, 0, g)
+
+        for g in range(PASSES - 1):
+            transpose_x(1, g + 1)
+            if g == 0:
+                for i in range(KV):
+                    add_bias(H + i, 0)
+            interleave_w(0, g, True)
+            quantize_x(1, g)
+            quantize_w(0, g, g + 1)
+            for i in range(KV):
+                project(H + i, 1, g)
+        last = PASSES - 1
+        interleave_w(0, last, True)
+        finish_tables(0)
+        quantize_w(0, last, last + 1)
+        quantize_x(1, last)
+        for i in range(KV):
+            transpose_out(H + i, 0)
+        project_all(0, 0)
+        interleave_w(1, 1, False)
+        add_bias(0, 0)
+        for i in range(KV):
+            project(H + i, 1, last)
+        project_all(0, 1)
+        for i in range(KV):
+            add_bias(H + i, 1)
+        interleave_w(1, 2, False)
+        add_bias(0, 1)
+        interleave_w(1, 3, False)
+        rotate(H, 0)
+        interleave_w(1, 0, True)
+        rotate(H + 1, 0)
+        quantize_w(1, 0, 2)
+        finish_tables(1)
+        for i in range(KV):
+            transpose_out(H + i, 1)
+        rotate(H, 1)
+        quantize_w(1, 2, PASSES)
+        add_products(H, 0, TOK)
+        rotate(H + 1, 1)
+        interleave_w(2, 0, True)
+        add_products(H + 1, 0, TOK)
+        for i in range(KV):
+            store_head(H + i, 0, TOK)
+
+        names = list(range(Q_PAIRS)) + ["v"]
+        for head in range(1, H):
+            scalar_pair = head // 2 + 2
+            jobs = []
+            if scalar_pair < len(names):
+                jobs = [1, 2] if head % 2 == 0 else [3]
+                if head == 1:
+                    jobs = [1, 2, 3]
+            for hh in range(2):
+                project_all(head, hh)
+                add_bias(head, hh)
+                if jobs:
+                    interleave_w(names[scalar_pair], jobs.pop(0), False)
+            for g in jobs:
+                interleave_w(names[scalar_pair], g, False)
+            if head == H - 2:
+                for j in range(TOK):
+                    nc.scalar.activation(out=bv_masked[:, j, :], in_=bv_all[:], func=ACT.Copy, scale=mask_f32[:, j:j + 1])
+            done = head - 1
+            for hh in range(2):
+                transpose_out(done, hh)
+            for hh in range(2):
+                rotate(done, hh)
+            if done % 2 == 0 and done // 2 + 2 < len(names):
+                quantize_w(names[done // 2 + 2], 0, PASSES)
+            elif done % 2 == 1 and (done + 5) // 2 < len(names):
+                interleave_w(names[(done + 5) // 2], 0, True)
+            add_products(done, 0, TOK)
+            store_head(done, 0, TOK)
+            if done == 0:
+                for g in range(PASSES):
+                    load_w([6, 7], Wq, 6 * PAIR, g)
+            if done == 1:
+                for g in range(PASSES):
+                    load_w(["v"], Wv, 0, g)
+
+        project_v(0)
+        for hh in range(2):
+            transpose_out(H - 1, hh)
+        for b in range(1, 4):
+            project_v(b)
+        for hh in range(2):
+            rotate(H - 1, hh)
+            add_products(H - 1, hh * HALF_TOK, (hh + 1) * HALF_TOK)
+            store_head(H - 1, hh * HALF_TOK, (hh + 1) * HALF_TOK)
+        for b in range(4):
+            finish_v(b)

@@ -29,7 +29,8 @@ N_HALF = HALF_TOK * P
 PAIR = 2 * D
 HD = D // 2
 Q_PAIRS = H // 2
-NARROW_PAIRS = 4
+NARROW_PAIRS = 6
+VECTOR_HELPS_FROM = 4
 
 
 def tile_multiheadattention_pa_kernel(tc, x, cos, sin, mask, Wq, bq, Wk, bk, Wv, bv, out_0, out_1, out_2):
@@ -62,7 +63,7 @@ def tile_multiheadattention_pa_kernel(tc, x, cos, sin, mask, Wq, bq, Wk, bk, Wv,
 
         x_raw, x_grouped = {}, {}
         w_raw, w_grouped, w_codes, w_scales = {}, {}, {}, {}
-        acc, chan_major, tok_major, prod_a, prod_b = {}, {}, {}, {}, {}
+        acc, chan_major, tok_major, prod = {}, {}, {}, {}
 
         def load_x(hh, g):
             t = ring.tile([P, HALF_TOK, K_PASS], BF16, tag="raw_wide", bufs=8, name="x_raw")
@@ -90,13 +91,18 @@ def tile_multiheadattention_pa_kernel(tc, x, cos, sin, mask, Wq, bq, Wk, bk, Wv,
                 dst = rot_last[:, rows, cs, 0:hi - lo]
             nc.sync.dma_start(out=dst, in_=src)
 
-        def finish_tables(hh):
+        def finish_tables(hh, on_vector):
             lo, hi = SECTIONS[2]
             rows = slice(hh * TOK, (hh + 1) * TOK)
-            nc.vector.tensor_copy(out=rot[:].rearrange("p j (f c) d -> p (j f) c d", c=2)[:, rows, :, lo:hi],
-                                  in_=rot_last[:, rows, :, 0:hi - lo])
+            dst = rot[:].rearrange("p j (f c) d -> p (j f) c d", c=2)[:, rows, :, lo:hi]
+            src = rot_last[:, rows, :, 0:hi - lo]
             first_sin = rot[:, hh * HALF_TOK:(hh + 1) * HALF_TOK, 1, :]
-            nc.vector.tensor_scalar(out=first_sin, in0=first_sin, scalar1=-1.0, scalar2=None, op0=MULT)
+            if on_vector:
+                nc.vector.tensor_copy(out=dst, in_=src)
+                nc.vector.tensor_scalar(out=first_sin, in0=first_sin, scalar1=-1.0, scalar2=None, op0=MULT)
+            else:
+                nc.scalar.copy(out=dst, in_=src)
+                nc.scalar.activation(out=first_sin, in_=first_sin, func=ACT.Copy, scale=-1.0)
 
         def transpose_x(hh, g):
             words = x_raw[hh, g][:].rearrange("p j k -> p (j k)").bitcast(F32)
@@ -117,8 +123,8 @@ def tile_multiheadattention_pa_kernel(tc, x, cos, sin, mask, Wq, bq, Wk, bk, Wv,
         def interleave_w(pair, g, on_vector):
             if pair not in w_grouped:
                 w_grouped[pair] = ring.tile([P, PASSES, PAIR, PACK], BF16, tag="w_grouped", bufs=3, align_bytes=64, name="w_grouped")
-            dst = w_grouped[pair][:, g].rearrange("p (c i) t -> p c t i", i=4)
-            src = w_raw[pair, g].rearrange("p t (c i) -> p c t i", i=4)
+            dst = w_grouped[pair][:, g]
+            src = w_raw[pair, g].rearrange("p t n -> p n t")
             if on_vector:
                 nc.vector.tensor_copy(out=dst, in_=src)
             else:
@@ -132,59 +138,61 @@ def tile_multiheadattention_pa_kernel(tc, x, cos, sin, mask, Wq, bq, Wk, bk, Wv,
                                   scales=w_scales[pair][:, g0:g1].rearrange("p g n -> p (g n)"),
                                   in_=w_grouped[pair][:, g0:g1].rearrange("p g n t -> p (g n t)"))
 
-        def pair_of(head):
-            return ("k", head - H) if head >= H else (head // 2, head % 2)
-
-        def project(head, hh, g):
-            pair, i = pair_of(head)
+        def project(pair, i, hh, g):
             if g == 0:
-                acc[head, hh] = psum.tile([P, N_HALF], F32, tag="acc", name="acc")
+                acc[pair, i, hh] = psum.tile([P, N_HALF], F32, tag="acc", name="acc")
             cols = slice(i * D, (i + 1) * D)
-            nc.tensor.matmul_mx(out=acc[head, hh][:], lhsT=w_codes[pair][:, g, cols].bitcast(E4M3), lhsT_scale=w_scales[pair][:, g, cols],
+            nc.tensor.matmul_mx(out=acc[pair, i, hh][:], lhsT=w_codes[pair][:, g, cols].bitcast(E4M3), lhsT_scale=w_scales[pair][:, g, cols],
                                 rhs=x_codes[hh, g][:].bitcast(E5M2), rhs_scale=x_scales[hh, g][:],
                                 start=(g == 0), stop=(g == PASSES - 1))
 
-        def project_all(head, hh):
-            for g in range(PASSES):
-                project(head, hh, g)
+        def add_bias(pair, i, hh):
+            head = H + i if pair == "k" else 2 * pair + i
+            t = ring.tile([P, N_HALF], F32, tag="chan_major", bufs=8, name="chan_major")
+            nc.scalar.activation(out=t[:], in_=acc[pair, i, hh][:], func=ACT.Identity, bias=bias_cols[:, head:head + 1])
+            chan_major[pair, i, hh] = t
 
-        def add_bias(head, hh):
-            t = ring.tile([P, N_HALF], F32, tag="chan_major", bufs=6, name="chan_major")
-            nc.scalar.activation(out=t[:], in_=acc[head, hh][:], func=ACT.Identity, bias=bias_cols[:, head:head + 1])
-            chan_major[head, hh] = t
+        def project_pair(pair, hh, scalar_jobs=(None, None)):
+            for i in range(2):
+                for g in range(PASSES):
+                    project(pair, i, hh, g)
+                if scalar_jobs[i]:
+                    interleave_w(*scalar_jobs[i], False)
+                add_bias(pair, i, hh)
 
-        def transpose_out(head, hh):
-            bank = psum.tile([P, HALF_TOK, D], F32, tag="turned", name="out_bank")
-            for j in range(HALF_TOK):
-                nc.tensor.transpose(bank[:, j, :], chan_major[head, hh][:, j * P:(j + 1) * P], ident[:])
-            tok_major[head, hh] = bank
+        def transpose_out(pair, hh):
+            for i in range(2):
+                bank = psum.tile([P, HALF_TOK, D], F32, tag="turned", name="out_bank")
+                for j in range(HALF_TOK):
+                    nc.tensor.transpose(bank[:, j, :], chan_major[pair, i, hh][:, j * P:(j + 1) * P], ident[:])
+                tok_major[pair, i, hh] = bank
 
-        def rotate(head, hh):
-            if hh == 0:
-                prod_a[head] = ring.tile([P, TOK, 2, HD], F32, tag="prod_a", bufs=6, name="prod_a")
-                prod_b[head] = ring.tile([P, TOK, 2, HD], F32, tag="prod_b", bufs=3, name="prod_b")
-            bank = tok_major[head, hh]
+        def rotate(pair, hh, heads=(0, 1)):
+            if (pair, hh, 0) not in prod:
+                prod[pair, hh, 0] = ring.tile([P, 2, HALF_TOK, 2, HD], F32, tag="prod_first", bufs=7, name="prod_first")
+                prod[pair, hh, 1] = ring.tile([P, 2, HALF_TOK, 2, HD], F32, tag="prod_second", bufs=3, name="prod_second")
             j0 = hh * HALF_TOK
-            for prod, f, slots in ((prod_a[head], 0, slice(0, 4, 3)), (prod_b[head], 1, slice(1, 3))):
-                feats = slice(f * HD, (f + 1) * HD)
-                if head < H:
-                    nc.vector.tensor_tensor(out=prod[:, j0:j0 + HALF_TOK],
-                                            in0=bank[:, :, feats].unsqueeze(2).to_broadcast([P, HALF_TOK, 2, HD]),
-                                            in1=rot[:, j0:j0 + HALF_TOK, slots, :], op=MULT)
-                else:
-                    for j in range(j0, j0 + HALF_TOK):
-                        nc.vector.scalar_tensor_tensor(out=prod[:, j], in0=bank[:, j - j0, feats].unsqueeze(1).to_broadcast([P, 2, HD]),
-                                                       scalar=mask_f32[:, j:j + 1], in1=rot[:, j, slots, :], op0=MULT, op1=MULT)
+            for i in heads:
+                bank = tok_major[pair, i, hh]
+                for f, slots in enumerate((slice(0, 4, 3), slice(1, 3))):
+                    feats = slice(f * HD, (f + 1) * HD)
+                    dst = prod[pair, hh, f][:, i]
+                    if pair != "k":
+                        nc.vector.tensor_tensor(out=dst, in0=bank[:, :, feats].unsqueeze(2).to_broadcast([P, HALF_TOK, 2, HD]),
+                                                in1=rot[:, j0:j0 + HALF_TOK, slots, :], op=MULT)
+                    else:
+                        for j in range(HALF_TOK):
+                            nc.vector.scalar_tensor_tensor(out=dst[:, j], in0=bank[:, j, feats].unsqueeze(1).to_broadcast([P, 2, HD]),
+                                                           scalar=mask_f32[:, j0 + j:j0 + j + 1], in1=rot[:, j0 + j, slots, :],
+                                                           op0=MULT, op1=MULT)
 
-        def add_products(head, j0, j1):
-            a = prod_a[head][:, j0:j1].rearrange("p j f d -> p (j f d)")
-            b = prod_b[head][:, j0:j1].rearrange("p j f d -> p (j f d)")
-            nc.gpsimd.tensor_tensor(out=a, in0=a, in1=b, op=ADD)
-
-        def store_head(head, j0, j1):
-            dst = out_1[0, head - H] if head >= H else out_0[0, head]
-            nc.sync.dma_start(out=dst.rearrange("(p j) d -> p j d", j=TOK)[:, j0:j1, :],
-                              in_=prod_a[head][:, j0:j1].rearrange("p j f d -> p j (f d)"))
+        def add_and_store(engine, pair, hh, i0=0, i1=2):
+            a = prod[pair, hh, 0][:, i0:i1].rearrange("p i j f d -> p (i j f d)")
+            b = prod[pair, hh, 1][:, i0:i1].rearrange("p i j f d -> p (i j f d)")
+            engine.tensor_tensor(out=a, in0=a, in1=b, op=ADD)
+            heads = out_1[0] if pair == "k" else out_0[0, 2 * pair:2 * pair + 2]
+            dst = heads.rearrange("h (p j) d -> p h j d", j=TOK)[:, i0:i1, hh * HALF_TOK:(hh + 1) * HALF_TOK, :]
+            nc.sync.dma_start(out=dst, in_=prod[pair, hh, 0][:, i0:i1].rearrange("p i j f d -> p i j (f d)"))
 
         def project_v(b):
             bank = psum.tile([P, 2, PAIR], F32, tag="acc", name="v_acc")
@@ -220,30 +228,21 @@ def tile_multiheadattention_pa_kernel(tc, x, cos, sin, mask, Wq, bq, Wk, bk, Wv,
         for g in range(2, PASSES):
             load_x(0, g)
             load_w(["k"], Wk, 0, g)
-        tables = [(cs, axis) for axis in range(3) for cs in range(2)]
         load_x(1, 0)
-        load_table(0, *tables[0])
         load_w([0], Wq, 0, 0)
-        load_table(0, *tables[1])
         load_x(1, 1)
-        load_table(0, *tables[2])
         load_w([0], Wq, 0, 1)
-        load_table(0, *tables[3])
         load_w([0], Wq, 0, 2)
-        load_table(0, *tables[4])
         load_x(1, 2)
-        load_table(0, *tables[5])
         load_w([0], Wq, 0, 3)
         load_x(1, 3)
-        for g in range(PASSES):
-            load_w([1], Wq, PAIR, g)
-        for cs, axis in tables:
-            load_table(1, cs, axis)
-        for pair in range(2, NARROW_PAIRS):
+        for pair in range(1, NARROW_PAIRS):
             for g in range(PASSES):
                 load_w([pair], Wq, pair * PAIR, g)
-        for g in range(PASSES):
-            load_w([4, 5], Wq, 4 * PAIR, g)
+            if pair in (2, 3):
+                for axis in range(3):
+                    for cs in range(2):
+                        load_table(pair - 2, cs, axis)
 
         transpose_x(0, 0)
         bias_bank = psum.tile([P, P], BF16, tag="acc", name="bias_bank")
@@ -265,96 +264,93 @@ def tile_multiheadattention_pa_kernel(tc, x, cos, sin, mask, Wq, bq, Wk, bk, Wv,
             quantize_x(0, g)
             quantize_w("k", g, g + 1)
             for i in range(KV):
-                project(H + i, 0, g)
+                project("k", i, 0, g)
 
         for g in range(PASSES - 1):
             transpose_x(1, g + 1)
             if g == 0:
                 for i in range(KV):
-                    add_bias(H + i, 0)
+                    add_bias("k", i, 0)
             interleave_w(0, g, True)
             quantize_x(1, g)
             quantize_w(0, g, g + 1)
             for i in range(KV):
-                project(H + i, 1, g)
+                project("k", i, 1, g)
         last = PASSES - 1
         interleave_w(0, last, True)
-        finish_tables(0)
         quantize_w(0, last, last + 1)
         quantize_x(1, last)
+        project_pair(0, 0)
         for i in range(KV):
-            transpose_out(H + i, 0)
-        project_all(0, 0)
-        interleave_w(1, 1, False)
-        add_bias(0, 0)
-        for i in range(KV):
-            project(H + i, 1, last)
-        project_all(0, 1)
-        for i in range(KV):
-            add_bias(H + i, 1)
-        interleave_w(1, 2, False)
-        add_bias(0, 1)
-        interleave_w(1, 3, False)
-        rotate(H, 0)
-        interleave_w(1, 0, True)
-        rotate(H + 1, 0)
+            project("k", i, 1, last)
+            add_bias("k", i, 1)
+        transpose_out("k", 0)
+        for g in range(3):
+            interleave_w(1, g, True)
         quantize_w(1, 0, 2)
-        finish_tables(1)
-        for i in range(KV):
-            transpose_out(H + i, 1)
-        rotate(H, 1)
-        quantize_w(1, 2, PASSES)
-        add_products(H, 0, TOK)
-        rotate(H + 1, 1)
+        interleave_w(1, 3, True)
         interleave_w(2, 0, True)
-        add_products(H + 1, 0, TOK)
-        for i in range(KV):
-            store_head(H + i, 0, TOK)
+        quantize_w(1, 2, PASSES)
+        interleave_w(2, 1, True)
+        interleave_w(2, 2, False)
+        interleave_w(2, 3, False)
+        project_pair(0, 1)
+        quantize_w(2, 0, PASSES)
+        transpose_out(0, 0)
+        finish_tables(0, True)
+        project_pair(1, 0, [None, (3, 0)])
+        interleave_w(3, 1, False)
+        project_pair(1, 1, [None, (3, 2)])
+        interleave_w(3, 3, False)
+        rotate("k", 0)
+        add_and_store(nc.gpsimd, "k", 0)
+        transpose_out(1, 0)
+        rotate(0, 0)
+        add_and_store(nc.gpsimd, 0, 0)
+        transpose_out("k", 1)
+        finish_tables(1, False)
+        rotate(1, 0)
+        quantize_w(3, 0, PASSES)
+        add_and_store(nc.gpsimd, 1, 0)
 
         names = list(range(Q_PAIRS)) + ["v"]
-        for head in range(1, H):
-            scalar_pair = head // 2 + 2
-            jobs = []
-            if scalar_pair < len(names):
-                jobs = [1, 2] if head % 2 == 0 else [3]
-                if head == 1:
-                    jobs = [1, 2, 3]
-            for hh in range(2):
-                project_all(head, hh)
-                add_bias(head, hh)
-                if jobs:
-                    interleave_w(names[scalar_pair], jobs.pop(0), False)
-            for g in jobs:
-                interleave_w(names[scalar_pair], g, False)
-            if head == H - 2:
-                for j in range(TOK):
-                    nc.scalar.activation(out=bv_masked[:, j, :], in_=bv_all[:], func=ACT.Copy, scale=mask_f32[:, j:j + 1])
-            done = head - 1
-            for hh in range(2):
-                transpose_out(done, hh)
-            for hh in range(2):
-                rotate(done, hh)
-            if done % 2 == 0 and done // 2 + 2 < len(names):
-                quantize_w(names[done // 2 + 2], 0, PASSES)
-            elif done % 2 == 1 and (done + 5) // 2 < len(names):
-                interleave_w(names[(done + 5) // 2], 0, True)
-            add_products(done, 0, TOK)
-            store_head(done, 0, TOK)
-            if done == 0:
+        groups = [("k", 1), (0, 1), (1, 1)] + [(pair, hh) for pair in range(2, Q_PAIRS) for hh in range(2)]
+        for m in range(3, len(groups)):
+            pair, hh = groups[m]
+            ahead = pair + 2
+            vector_helps = ahead >= VECTOR_HELPS_FROM
+            if ahead < len(names):
+                if vector_helps and hh == 0:
+                    project_pair(pair, hh, [None, (names[ahead], 1)])
+                else:
+                    interleave_w(names[ahead], 2 * hh, False)
+                    project_pair(pair, hh, [None, (names[ahead], 2 * hh + 1)])
+            else:
+                project_pair(pair, hh)
+            rotate(*groups[m - 3])
+            if hh == 0 and pair > 2:
+                quantize_w(names[pair + 1], 0, PASSES)
+            elif hh == 1 and vector_helps and ahead < len(names):
+                interleave_w(names[ahead], 0, True)
+            add_and_store(nc.gpsimd, *groups[m - 3])
+            transpose_out(*groups[m - 2])
+            if m == 3:
                 for g in range(PASSES):
                     load_w([6, 7], Wq, 6 * PAIR, g)
-            if done == 1:
+            if m == 5:
                 for g in range(PASSES):
                     load_w(["v"], Wv, 0, g)
 
-        project_v(0)
-        for hh in range(2):
-            transpose_out(H - 1, hh)
-        for b in range(1, 4):
-            project_v(b)
-        for hh in range(2):
-            rotate(H - 1, hh)
-            add_products(H - 1, hh * HALF_TOK, (hh + 1) * HALF_TOK)
-            store_head(H - 1, hh * HALF_TOK, (hh + 1) * HALF_TOK)
-        for b in range(4):
-            finish_v(b)
+        for j in range(TOK):
+            nc.scalar.activation(out=bv_masked[:, j, :], in_=bv_all[:], func=ACT.Copy, scale=mask_f32[:, j:j + 1])
+        for half in range(2):
+            for b in (2 * half, 2 * half + 1):
+                project_v(b)
+            rotate(*groups[half - 3])
+            transpose_out(*groups[half - 2])
+            for b in (2 * half, 2 * half + 1):
+                finish_v(b)
+            add_and_store(nc.gpsimd, *groups[half - 3])
+        for i, engine in enumerate((nc.gpsimd, nc.vector)):
+            rotate(*groups[-1], heads=(i,))
+            add_and_store(engine, *groups[-1], i, i + 1)

@@ -29,8 +29,7 @@ N_HALF = HALF_TOK * P
 PAIR = 2 * D
 HD = D // 2
 Q_PAIRS = H // 2
-NARROW_PAIRS = 6
-VECTOR_HELPS_FROM = 4
+ALL_STEPS = ((0, 0), (0, 1), (1, 0), (1, 1))
 
 
 def tile_multiheadattention_pa_kernel(tc, x, cos, sin, mask, Wq, bq, Wk, bk, Wv, bv, out_0, out_1, out_2):
@@ -46,14 +45,11 @@ def tile_multiheadattention_pa_kernel(tc, x, cos, sin, mask, Wq, bq, Wk, bk, Wv,
         ident = keep.tile([P, P], F32)
         ident_bf = keep.tile([P, P], BF16)
         bias_rows = keep.tile([P, D], BF16)
-        bias_cols = keep.tile([P, H + KV], F32)
-        bv_all = keep.tile([P, PAIR], F32)
-        bv_masked = keep.tile([P, TOK, PAIR], F32)
+        bias_cols = keep.tile([P, H + 2 * KV], F32)
         mask_bf = keep.tile([P, TOK], BF16)
         mask_f32 = keep.tile([P, TOK], F32)
         rot = keep.tile([P, TOK, 4, HD], BF16)
         rot_last = keep.tile([P, 2 * TOK, 2, 32], BF16)
-        v_out = keep.tile([P, KV, TOK, D], F32)
         x_codes = {}
         x_scales = {}
         for hh in range(2):
@@ -61,25 +57,35 @@ def tile_multiheadattention_pa_kernel(tc, x, cos, sin, mask, Wq, bq, Wk, bk, Wv,
                 x_codes[hh, g] = keep.tile([P, N_HALF], U32, align_bytes=64, name="x_codes_%d_%d" % (hh, g))
                 x_scales[hh, g] = keep.tile([P, N_HALF], U8, align_bytes=64, name="x_scales_%d_%d" % (hh, g))
 
+        first_head = {pair: 2 * pair for pair in range(Q_PAIRS)}
+        first_head["k"] = H
+        first_head["v"] = H + KV
         x_raw, x_grouped = {}, {}
         w_raw, w_grouped, w_codes, w_scales = {}, {}, {}, {}
         acc, chan_major, tok_major, prod = {}, {}, {}, {}
 
-        def load_x(hh, g):
-            t = ring.tile([P, HALF_TOK, K_PASS], BF16, tag="raw_wide", bufs=8, name="x_raw")
-            nc.sync.dma_start(out=t[:], in_=x_tok[:, hh * HALF_TOK:(hh + 1) * HALF_TOK, g * K_PASS:(g + 1) * K_PASS])
-            x_raw[hh, g] = t
+        def load_x(hh, c):
+            t = ring.tile([P, HIDDEN], BF16, tag="raw_wide", bufs=12, name="x_raw")
+            if hh == 0:
+                nc.sync.dma_start(out=t[:].rearrange("p (j k) -> p j k", j=HALF_TOK), in_=x_tok[:, 0:HALF_TOK, c * K_PASS:(c + 1) * K_PASS])
+            else:
+                nc.sync.dma_start(out=t[:], in_=x_tok[:, HALF_TOK + c, :])
+            x_raw[hh, c] = t
 
         def load_w(pairs, W, col0, g):
             width = PAIR * len(pairs)
             if len(pairs) == 1:
-                t = ring.tile([P, PACK, width], BF16, tag="raw_narrow", bufs=16, name="w_narrow")
+                t = ring.tile([P, PACK, width], BF16, tag="raw_narrow", bufs=4, name="w_narrow")
             else:
-                t = ring.tile([P, PACK, width], BF16, tag="raw_wide", bufs=8, name="w_wide")
+                t = ring.tile([P, PACK, width], BF16, tag="raw_wide", bufs=12, name="w_wide")
             rows = W[g * K_PASS:(g + 1) * K_PASS, col0:col0 + width]
             nc.sync.dma_start(out=t[:], in_=rows.rearrange("(p j) n -> p j n", j=PACK))
             for i, pair in enumerate(pairs):
                 w_raw[pair, g] = t[:, :, i * PAIR:(i + 1) * PAIR]
+
+        def load_wq(pair):
+            for g in range(PASSES):
+                load_w([pair, pair + 1], Wq, pair * PAIR, g)
 
         def load_table(hh, cs, axis):
             lo, hi = SECTIONS[axis]
@@ -105,7 +111,7 @@ def tile_multiheadattention_pa_kernel(tc, x, cos, sin, mask, Wq, bq, Wk, bk, Wv,
                 nc.scalar.activation(out=first_sin, in_=first_sin, func=ACT.Copy, scale=-1.0)
 
         def transpose_x(hh, g):
-            words = x_raw[hh, g][:].rearrange("p j k -> p (j k)").bitcast(F32)
+            words = x_raw[hh, g][:].bitcast(F32)
             grouped = ring.tile([P, N_HALF * PACK], BF16, tag="x_grouped", bufs=3, align_bytes=64, name="x_grouped")
             x_grouped[hh, g] = grouped
             for b in range(2):
@@ -117,8 +123,14 @@ def tile_multiheadattention_pa_kernel(tc, x, cos, sin, mask, Wq, bq, Wk, bk, Wv,
                 dst = grouped[:, b * 2 * P * PACK:(b + 1) * 2 * P * PACK].bitcast(F32)
                 nc.scalar.copy(out=dst.rearrange("p (j r u) -> p j r u", j=2, u=2), in_=bank[:].rearrange("p j u r -> p j r u"))
 
-        def quantize_x(hh, g):
-            nc.vector.quantize_mx(out=x_codes[hh, g][:].bitcast(E5M2), scales=x_scales[hh, g][:], in_=x_grouped[hh, g][:])
+        def quantize_x(hh, c):
+            if hh == 0:
+                nc.vector.quantize_mx(out=x_codes[0, c][:].bitcast(E5M2), scales=x_scales[0, c][:], in_=x_grouped[0, c][:])
+            else:
+                toks = slice(c * P, (c + 1) * P)
+                for g in range(PASSES):
+                    nc.vector.quantize_mx(out=x_codes[1, g][:, toks].bitcast(E5M2), scales=x_scales[1, g][:, toks],
+                                          in_=x_grouped[1, c][:, g * K_PASS:(g + 1) * K_PASS])
 
         def interleave_w(pair, g, on_vector):
             if pair not in w_grouped:
@@ -146,9 +158,20 @@ def tile_multiheadattention_pa_kernel(tc, x, cos, sin, mask, Wq, bq, Wk, bk, Wv,
                                 rhs=x_codes[hh, g][:].bitcast(E5M2), rhs_scale=x_scales[hh, g][:],
                                 start=(g == 0), stop=(g == PASSES - 1))
 
+        def project_keys_second_half(j):
+            toks = slice(j * P, (j + 1) * P)
+            for i in range(KV):
+                if j == 0:
+                    acc["k", i, 1] = psum.tile([P, N_HALF], F32, tag="acc", name="acc")
+                cols = slice(i * D, (i + 1) * D)
+                for g in range(PASSES):
+                    nc.tensor.matmul_mx(out=acc["k", i, 1][:, toks], lhsT=w_codes["k"][:, g, cols].bitcast(E4M3), lhsT_scale=w_scales["k"][:, g, cols],
+                                        rhs=x_codes[1, g][:, toks].bitcast(E5M2), rhs_scale=x_scales[1, g][:, toks],
+                                        start=(g == 0), stop=(g == PASSES - 1))
+
         def add_bias(pair, i, hh):
-            head = H + i if pair == "k" else 2 * pair + i
-            t = ring.tile([P, N_HALF], F32, tag="chan_major", bufs=8, name="chan_major")
+            head = first_head[pair] + i
+            t = ring.tile([P, N_HALF], F32, tag="chan_major", bufs=10, name="chan_major")
             nc.scalar.activation(out=t[:], in_=acc[pair, i, hh][:], func=ACT.Identity, bias=bias_cols[:, head:head + 1])
             chan_major[pair, i, hh] = t
 
@@ -160,31 +183,30 @@ def tile_multiheadattention_pa_kernel(tc, x, cos, sin, mask, Wq, bq, Wk, bk, Wv,
                     interleave_w(*scalar_jobs[i], False)
                 add_bias(pair, i, hh)
 
-        def transpose_out(pair, hh):
-            for i in range(2):
-                bank = psum.tile([P, HALF_TOK, D], F32, tag="turned", name="out_bank")
-                for j in range(HALF_TOK):
-                    nc.tensor.transpose(bank[:, j, :], chan_major[pair, i, hh][:, j * P:(j + 1) * P], ident[:])
-                tok_major[pair, i, hh] = bank
+        def transpose_out(pair, hh, tag="turned"):
+            for b in range(2):
+                bank = psum.tile([P, HALF_TOK, D], F32, tag=tag, name="out_bank")
+                for s in range(HALF_TOK):
+                    nc.tensor.transpose(bank[:, s, :], chan_major[pair, b, hh][:, s * P:(s + 1) * P], ident[:])
+                tok_major[pair, b, hh] = bank
 
-        def rotate(pair, hh, heads=(0, 1)):
+        def rotate(pair, hh, steps=ALL_STEPS):
             if (pair, hh, 0) not in prod:
-                prod[pair, hh, 0] = ring.tile([P, 2, HALF_TOK, 2, HD], F32, tag="prod_first", bufs=7, name="prod_first")
+                prod[pair, hh, 0] = ring.tile([P, 2, HALF_TOK, 2, HD], F32, tag="prod_first", bufs=10, name="prod_first")
                 prod[pair, hh, 1] = ring.tile([P, 2, HALF_TOK, 2, HD], F32, tag="prod_second", bufs=3, name="prod_second")
             j0 = hh * HALF_TOK
-            for i in heads:
-                bank = tok_major[pair, i, hh]
-                for f, slots in enumerate((slice(0, 4, 3), slice(1, 3))):
-                    feats = slice(f * HD, (f + 1) * HD)
-                    dst = prod[pair, hh, f][:, i]
-                    if pair != "k":
-                        nc.vector.tensor_tensor(out=dst, in0=bank[:, :, feats].unsqueeze(2).to_broadcast([P, HALF_TOK, 2, HD]),
-                                                in1=rot[:, j0:j0 + HALF_TOK, slots, :], op=MULT)
-                    else:
-                        for j in range(HALF_TOK):
-                            nc.vector.scalar_tensor_tensor(out=dst[:, j], in0=bank[:, j, feats].unsqueeze(1).to_broadcast([P, 2, HD]),
-                                                           scalar=mask_f32[:, j0 + j:j0 + j + 1], in1=rot[:, j0 + j, slots, :],
-                                                           op0=MULT, op1=MULT)
+            for b, f in steps:
+                bank = tok_major[pair, b, hh]
+                slots = (slice(0, 4, 3), slice(1, 3))[f]
+                feats = slice(f * HD, (f + 1) * HD)
+                if pair != "k":
+                    nc.vector.tensor_tensor(out=prod[pair, hh, f][:, b], in0=bank[:, :, feats].unsqueeze(2).to_broadcast([P, HALF_TOK, 2, HD]),
+                                            in1=rot[:, j0:j0 + HALF_TOK, slots, :], op=MULT)
+                else:
+                    for j in range(HALF_TOK):
+                        nc.vector.scalar_tensor_tensor(out=prod[pair, hh, f][:, b, j], in0=bank[:, j, feats].unsqueeze(1).to_broadcast([P, 2, HD]),
+                                                       scalar=mask_f32[:, j0 + j:j0 + j + 1], in1=rot[:, j0 + j, slots, :],
+                                                       op0=MULT, op1=MULT)
 
         def add_and_store(engine, pair, hh, i0=0, i1=2):
             a = prod[pair, hh, 0][:, i0:i1].rearrange("p i j f d -> p (i j f d)")
@@ -194,25 +216,13 @@ def tile_multiheadattention_pa_kernel(tc, x, cos, sin, mask, Wq, bq, Wk, bk, Wv,
             dst = heads.rearrange("h (p j) d -> p h j d", j=TOK)[:, i0:i1, hh * HALF_TOK:(hh + 1) * HALF_TOK, :]
             nc.sync.dma_start(out=dst, in_=prod[pair, hh, 0][:, i0:i1].rearrange("p i j f d -> p i j (f d)"))
 
-        def project_v(b):
-            bank = psum.tile([P, 2, PAIR], F32, tag="acc", name="v_acc")
-            acc["v", b] = bank
-            for jj in range(2):
-                hh, j = divmod(2 * b + jj, HALF_TOK)
-                toks = slice(j * P, (j + 1) * P)
-                for g in range(PASSES):
-                    nc.tensor.matmul_mx(out=bank[:, jj, :], lhsT=x_codes[hh, g][:, toks].bitcast(E5M2), lhsT_scale=x_scales[hh, g][:, toks],
-                                        rhs=w_codes["v"][:, g, :].bitcast(E4M3), rhs_scale=w_scales["v"][:, g, :],
-                                        start=(g == 0), stop=(g == PASSES - 1))
-
-        def finish_v(b):
-            for jj in range(2):
-                j = 2 * b + jj
-                nc.vector.scalar_tensor_tensor(out=v_out[:, :, j, :], in0=acc["v", b][:, jj, :].rearrange("p (h d) -> p h d", h=KV),
-                                               scalar=mask_f32[:, j:j + 1], in1=bv_masked[:, j, :].rearrange("p (h d) -> p h d", h=KV),
-                                               op0=MULT, op1=ADD)
-            nc.sync.dma_start(out=out_2[0].rearrange("h (p j) d -> p h j d", j=TOK)[:, :, 2 * b:2 * b + 2, :],
-                              in_=v_out[:, :, 2 * b:2 * b + 2, :])
+        def finish_v(hh):
+            v_out = ring.tile([P, KV, HALF_TOK, D], F32, tag="prod_first", bufs=10, name="v_out")
+            for i in range(KV):
+                for j in range(HALF_TOK):
+                    tok = hh * HALF_TOK + j
+                    nc.scalar.activation(out=v_out[:, i, j, :], in_=tok_major["v", i, hh][:, j, :], func=ACT.Copy, scale=mask_f32[:, tok:tok + 1])
+            nc.sync.dma_start(out=out_2[0].rearrange("h (p j) d -> p h j d", j=TOK)[:, :, hh * HALF_TOK:(hh + 1) * HALF_TOK, :], in_=v_out[:])
 
         make_identity(nc, ident[:])
         make_identity(nc, ident_bf[:])
@@ -228,30 +238,18 @@ def tile_multiheadattention_pa_kernel(tc, x, cos, sin, mask, Wq, bq, Wk, bk, Wv,
         for g in range(2, PASSES):
             load_x(0, g)
             load_w(["k"], Wk, 0, g)
-        load_x(1, 0)
-        load_w([0], Wq, 0, 0)
-        load_x(1, 1)
-        load_w([0], Wq, 0, 1)
-        load_w([0], Wq, 0, 2)
-        load_x(1, 2)
-        load_w([0], Wq, 0, 3)
-        load_x(1, 3)
-        for pair in range(1, NARROW_PAIRS):
-            for g in range(PASSES):
-                load_w([pair], Wq, pair * PAIR, g)
-            if pair in (2, 3):
-                for axis in range(3):
-                    for cs in range(2):
-                        load_table(pair - 2, cs, axis)
+        for c in range(PASSES):
+            load_x(1, c)
+            load_w([0, 1], Wq, 0, c)
+        for hh in range(2):
+            for axis in range(3):
+                for cs in range(2):
+                    load_table(hh, cs, axis)
+            load_wq(2 + 2 * hh)
 
         transpose_x(0, 0)
         bias_bank = psum.tile([P, P], BF16, tag="acc", name="bias_bank")
         nc.tensor.transpose(bias_bank[:], bias_rows[:], ident_bf[:])
-        bv_bank = psum.tile([P, PAIR], F32, tag="acc", name="bv_bank")
-        for i in range(KV):
-            row = H + KV + i
-            nc.tensor.matmul(bv_bank[:, i * D:(i + 1) * D], lhsT=ident_bf[:, row:row + 1].to_broadcast([P, P]), rhs=bias_rows[:],
-                             start=True, stop=True)
         for g in range(PASSES):
             if g + 1 < PASSES:
                 transpose_x(0, g + 1)
@@ -259,98 +257,103 @@ def tile_multiheadattention_pa_kernel(tc, x, cos, sin, mask, Wq, bq, Wk, bk, Wv,
                 transpose_x(1, 0)
             interleave_w("k", g, True)
             if g == 0:
-                nc.vector.tensor_copy(out=bias_cols[:], in_=bias_bank[:, 0:H + KV])
-                nc.vector.tensor_copy(out=bv_all[:], in_=bv_bank[:])
+                nc.vector.tensor_copy(out=bias_cols[:], in_=bias_bank[:, 0:H + 2 * KV])
             quantize_x(0, g)
             quantize_w("k", g, g + 1)
             for i in range(KV):
                 project("k", i, 0, g)
 
-        for g in range(PASSES - 1):
-            transpose_x(1, g + 1)
-            if g == 0:
+        last = PASSES - 1
+        for c in range(last):
+            if c == 0:
                 for i in range(KV):
                     add_bias("k", i, 0)
-            interleave_w(0, g, True)
-            quantize_x(1, g)
-            quantize_w(0, g, g + 1)
-            for i in range(KV):
-                project("k", i, 1, g)
-        last = PASSES - 1
+            interleave_w(0, c, True)
+            quantize_x(1, c)
+            quantize_w(0, c, c + 1)
+            interleave_w(1, c, c == 0)
+            transpose_x(1, c + 1)
+            project_keys_second_half(c)
+        quantize_w(1, 0, 2)
         interleave_w(0, last, True)
         quantize_w(0, last, last + 1)
         quantize_x(1, last)
-        project_pair(0, 0)
-        for i in range(KV):
-            project("k", i, 1, last)
-            add_bias("k", i, 1)
-        transpose_out("k", 0)
-        for g in range(3):
-            interleave_w(1, g, True)
-        quantize_w(1, 0, 2)
-        interleave_w(1, 3, True)
-        interleave_w(2, 0, True)
+        interleave_w(1, last, False)
         quantize_w(1, 2, PASSES)
-        interleave_w(2, 1, True)
-        interleave_w(2, 2, False)
-        interleave_w(2, 3, False)
-        project_pair(0, 1)
-        quantize_w(2, 0, PASSES)
-        transpose_out(0, 0)
         finish_tables(0, True)
-        project_pair(1, 0, [None, (3, 0)])
-        interleave_w(3, 1, False)
-        project_pair(1, 1, [None, (3, 2)])
-        interleave_w(3, 3, False)
-        rotate("k", 0)
-        add_and_store(nc.gpsimd, "k", 0)
-        transpose_out(1, 0)
-        rotate(0, 0)
-        add_and_store(nc.gpsimd, 0, 0)
-        transpose_out("k", 1)
-        finish_tables(1, False)
-        rotate(1, 0)
-        quantize_w(3, 0, PASSES)
-        add_and_store(nc.gpsimd, 1, 0)
 
-        names = list(range(Q_PAIRS)) + ["v"]
-        groups = [("k", 1), (0, 1), (1, 1)] + [(pair, hh) for pair in range(2, Q_PAIRS) for hh in range(2)]
-        for m in range(3, len(groups)):
-            pair, hh = groups[m]
-            ahead = pair + 2
-            vector_helps = ahead >= VECTOR_HELPS_FROM
-            if ahead < len(names):
-                if vector_helps and hh == 0:
-                    project_pair(pair, hh, [None, (names[ahead], 1)])
-                else:
-                    interleave_w(names[ahead], 2 * hh, False)
-                    project_pair(pair, hh, [None, (names[ahead], 2 * hh + 1)])
+        names = list(range(Q_PAIRS - 1)) + ["v", Q_PAIRS - 1]
+        groups = [("k", 0), (0, 0), (1, 0), (2, 0), ("k", 1), (0, 1), (1, 1), (2, 1)]
+        groups += [(pair, hh) for pair in range(3, Q_PAIRS) for hh in range(2)]
+
+        project_pair(0, 0)
+        project_keys_second_half(last)
+        for i in range(KV):
+            add_bias("k", i, 1)
+        transpose_out(*groups[0])
+        project_pair(1, 0)
+        transpose_out(*groups[1])
+        interleave_w(3, 0, False)
+        project_pair(0, 1, [None, (2, 1)])
+        interleave_w(2, 2, False)
+        project_pair(1, 1)
+        for g in (1, 2):
+            interleave_w(3, g, False)
+        rotate(*groups[0])
+        interleave_w(2, 0, True)
+        add_and_store(nc.gpsimd, *groups[0])
+        transpose_out(*groups[2])
+        rotate(*groups[1], steps=ALL_STEPS[:3])
+        interleave_w(2, 3, True)
+        quantize_w(2, 0, PASSES)
+        rotate(*groups[1], steps=ALL_STEPS[3:])
+        add_and_store(nc.gpsimd, *groups[1])
+        load_wq(6)
+        rotate(*groups[2])
+        interleave_w(3, 3, True)
+        add_and_store(nc.gpsimd, *groups[2])
+        project_pair(2, 0)
+        for i in range(2):
+            for g in range(PASSES):
+                project(2, i, 1, g)
+            add_bias(2, i, 1)
+            transpose_out(*groups[3 + i])
+        finish_tables(1, False)
+        for g in range(1, PASSES):
+            interleave_w(4, g, False)
+        rotate(*groups[3])
+        quantize_w(3, 0, PASSES)
+        add_and_store(nc.gpsimd, *groups[3])
+        transpose_out(*groups[5])
+        rotate(*groups[4])
+        interleave_w(4, 0, True)
+        add_and_store(nc.gpsimd, *groups[4])
+
+        first = names.index(3)
+        for n in range(2 * (len(names) - first)):
+            at, hh = first + n // 2, n % 2
+            ahead = names[at + 2] if at + 2 < len(names) else None
+            if ahead is None:
+                project_pair(names[at], hh)
+            elif hh == 0:
+                project_pair(names[at], hh, [None, (ahead, 1)])
             else:
-                project_pair(pair, hh)
-            rotate(*groups[m - 3])
-            if hh == 0 and pair > 2:
-                quantize_w(names[pair + 1], 0, PASSES)
-            elif hh == 1 and vector_helps and ahead < len(names):
-                interleave_w(names[ahead], 0, True)
-            add_and_store(nc.gpsimd, *groups[m - 3])
-            transpose_out(*groups[m - 2])
-            if m == 3:
-                for g in range(PASSES):
-                    load_w([6, 7], Wq, 6 * PAIR, g)
-            if m == 5:
+                interleave_w(ahead, 2, False)
+                project_pair(names[at], hh, [None, (ahead, 3)])
+            rotate(*groups[n + 5])
+            if hh == 0 and at + 1 < len(names):
+                quantize_w(names[at + 1], 0, PASSES)
+            elif hh == 1 and ahead is not None:
+                interleave_w(ahead, 0, True)
+            for v_half in range(2):
+                if n == 2 * (names.index("v") - first) + 1 + v_half:
+                    transpose_out("v", v_half, tag="acc")
+                    finish_v(v_half)
+            add_and_store(nc.gpsimd, *groups[n + 5])
+            transpose_out(*groups[n + 6])
+            if n == 0:
                 for g in range(PASSES):
                     load_w(["v"], Wv, 0, g)
-
-        for j in range(TOK):
-            nc.scalar.activation(out=bv_masked[:, j, :], in_=bv_all[:], func=ACT.Copy, scale=mask_f32[:, j:j + 1])
-        for half in range(2):
-            for b in (2 * half, 2 * half + 1):
-                project_v(b)
-            rotate(*groups[half - 3])
-            transpose_out(*groups[half - 2])
-            for b in (2 * half, 2 * half + 1):
-                finish_v(b)
-            add_and_store(nc.gpsimd, *groups[half - 3])
-        for i, engine in enumerate((nc.gpsimd, nc.vector)):
-            rotate(*groups[-1], heads=(i,))
-            add_and_store(engine, *groups[-1], i, i + 1)
+        rotate(*groups[-1])
+        for i in range(2):
+            add_and_store(nc.vector, *groups[-1], i, i + 1)

@@ -29,7 +29,6 @@ N_HALF = HALF_TOK * P
 PAIR = 2 * D
 HD = D // 2
 Q_PAIRS = H // 2
-ALL_STEPS = ((0, 0), (0, 1), (1, 0), (1, 1))
 
 
 def tile_multiheadattention_pa_kernel(tc, x, cos, sin, mask, Wq, bq, Wk, bk, Wv, bv, out_0, out_1, out_2):
@@ -49,7 +48,7 @@ def tile_multiheadattention_pa_kernel(tc, x, cos, sin, mask, Wq, bq, Wk, bk, Wv,
         mask_bf = keep.tile([P, TOK], BF16)
         mask_f32 = keep.tile([P, TOK], F32)
         rot = keep.tile([P, TOK, 4, HD], BF16)
-        rot_last = keep.tile([P, 2 * TOK, 2, 32], BF16)
+        rot_last = keep.tile([P, TOK, 4, 32], BF16)
         x_codes = {}
         x_scales = {}
         for hh in range(2):
@@ -60,7 +59,7 @@ def tile_multiheadattention_pa_kernel(tc, x, cos, sin, mask, Wq, bq, Wk, bk, Wv,
         first_head = {pair: 2 * pair for pair in range(Q_PAIRS)}
         first_head["k"] = H
         first_head["v"] = H + KV
-        x_raw, x_grouped = {}, {}
+        x_raw, x_grouped, rot_masked = {}, {}, {}
         w_raw, w_grouped, w_codes, w_scales = {}, {}, {}, {}
         acc, chan_major, tok_major, prod = {}, {}, {}, {}
 
@@ -87,28 +86,35 @@ def tile_multiheadattention_pa_kernel(tc, x, cos, sin, mask, Wq, bq, Wk, bk, Wv,
             for g in range(PASSES):
                 load_w([pair, pair + 1], Wq, pair * PAIR, g)
 
-        def load_table(hh, cs, axis):
-            lo, hi = SECTIONS[axis]
-            rows = slice(hh * TOK, (hh + 1) * TOK)
-            src = (cos, sin)[cs][axis, 0].rearrange("(p j) (f d) -> p (j f) d", j=TOK, f=2)[:, rows, lo:hi]
-            if axis < 2:
-                dst = rot[:].rearrange("p j (f c) d -> p (j f) c d", c=2)[:, rows, cs, lo:hi]
-            else:
-                dst = rot_last[:, rows, cs, 0:hi - lo]
-            nc.sync.dma_start(out=dst, in_=src)
+        def load_tables(hh):
+            toks = slice(hh * HALF_TOK, (hh + 1) * HALF_TOK)
+            order = [(2, slot) for slot in range(4)] + [(axis, slot) for slot in (2, 0, 1, 3) for axis in range(2)]
+            for axis, slot in order:
+                lo, hi = SECTIONS[axis]
+                table, f = ((cos, 0), (sin, 1), (sin, 0), (cos, 1))[slot]
+                src = table[axis, 0].rearrange("(p j) (f d) -> p j f d", j=TOK, f=2)[:, toks, f, lo:hi]
+                dst = rot[:, toks, slot, lo:hi] if axis < 2 else rot_last[:, toks, slot, 0:hi - lo]
+                nc.sync.dma_start(out=dst, in_=src)
 
         def finish_tables(hh, on_vector):
             lo, hi = SECTIONS[2]
-            rows = slice(hh * TOK, (hh + 1) * TOK)
-            dst = rot[:].rearrange("p j (f c) d -> p (j f) c d", c=2)[:, rows, :, lo:hi]
-            src = rot_last[:, rows, :, 0:hi - lo]
-            first_sin = rot[:, hh * HALF_TOK:(hh + 1) * HALF_TOK, 1, :]
+            toks = slice(hh * HALF_TOK, (hh + 1) * HALF_TOK)
+            dst = rot[:, toks, :, lo:hi]
+            src = rot_last[:, toks, :, 0:hi - lo]
+            first_sin = rot[:, toks, 2, :]
             if on_vector:
                 nc.vector.tensor_copy(out=dst, in_=src)
                 nc.vector.tensor_scalar(out=first_sin, in0=first_sin, scalar1=-1.0, scalar2=None, op0=MULT)
             else:
                 nc.scalar.copy(out=dst, in_=src)
                 nc.scalar.activation(out=first_sin, in_=first_sin, func=ACT.Copy, scale=-1.0)
+
+        def mask_tables(engine, hh):
+            toks = slice(hh * HALF_TOK, (hh + 1) * HALF_TOK)
+            t = ring.tile([P, HALF_TOK, 4 * HD], F32, tag="rot_masked", bufs=1, name="rot_masked")
+            engine.tensor_tensor(out=t[:], in0=rot[:, toks].rearrange("p j s d -> p j (s d)"),
+                                 in1=mask_f32[:, toks].unsqueeze(2).to_broadcast([P, HALF_TOK, 4 * HD]), op=MULT)
+            rot_masked[hh] = t
 
         def transpose_x(hh, g):
             words = x_raw[hh, g][:].bitcast(F32)
@@ -190,34 +196,28 @@ def tile_multiheadattention_pa_kernel(tc, x, cos, sin, mask, Wq, bq, Wk, bk, Wv,
                     nc.tensor.transpose(bank[:, s, :], chan_major[pair, b, hh][:, s * P:(s + 1) * P], ident[:])
                 tok_major[pair, b, hh] = bank
 
-        def rotate(pair, hh, steps=ALL_STEPS):
-            if (pair, hh, 0) not in prod:
-                prod[pair, hh, 0] = ring.tile([P, 2, HALF_TOK, 2, HD], F32, tag="prod_first", bufs=10, name="prod_first")
-                prod[pair, hh, 1] = ring.tile([P, 2, HALF_TOK, 2, HD], F32, tag="prod_second", bufs=3, name="prod_second")
-            j0 = hh * HALF_TOK
-            for b, f in steps:
-                bank = tok_major[pair, b, hh]
-                slots = (slice(0, 4, 3), slice(1, 3))[f]
-                feats = slice(f * HD, (f + 1) * HD)
-                if pair != "k":
-                    nc.vector.tensor_tensor(out=prod[pair, hh, f][:, b], in0=bank[:, :, feats].unsqueeze(2).to_broadcast([P, HALF_TOK, 2, HD]),
-                                            in1=rot[:, j0:j0 + HALF_TOK, slots, :], op=MULT)
-                else:
-                    for j in range(HALF_TOK):
-                        nc.vector.scalar_tensor_tensor(out=prod[pair, hh, f][:, b, j], in0=bank[:, j, feats].unsqueeze(1).to_broadcast([P, 2, HD]),
-                                                       scalar=mask_f32[:, j0 + j:j0 + j + 1], in1=rot[:, j0 + j, slots, :],
-                                                       op0=MULT, op1=MULT)
+        def rotate(pair, hh, heads=(0, 1)):
+            if (pair, hh) not in prod:
+                prod[pair, hh] = ring.tile([P, 2, HALF_TOK, 2, D], F32, tag="prod", bufs=3, name="prod")
+            if pair == "k":
+                factors = rot_masked[hh][:].rearrange("p j (f r d) -> p (j f) r d", f=2, r=2)
+            else:
+                factors = rot[:, hh * HALF_TOK:(hh + 1) * HALF_TOK].rearrange("p j (f r) d -> p (j f) r d", f=2)
+            for i in heads:
+                halves = tok_major[pair, i, hh][:].rearrange("p j (f d) -> p (j f) d", f=2)
+                nc.vector.tensor_tensor(out=prod[pair, hh][:, i].rearrange("p j f (r d) -> p (j f) r d", r=2),
+                                        in0=halves.unsqueeze(2).to_broadcast([P, 2 * HALF_TOK, 2, HD]), in1=factors, op=MULT)
 
         def add_and_store(engine, pair, hh, i0=0, i1=2):
-            a = prod[pair, hh, 0][:, i0:i1].rearrange("p i j f d -> p (i j f d)")
-            b = prod[pair, hh, 1][:, i0:i1].rearrange("p i j f d -> p (i j f d)")
-            engine.tensor_tensor(out=a, in0=a, in1=b, op=ADD)
+            result = ring.tile([P, i1 - i0, HALF_TOK, D], F32, tag="result", bufs=9, name="result")
+            both = prod[pair, hh][:, i0:i1].rearrange("p i j f d -> p (i j) f d")
+            engine.tensor_tensor(out=result[:].rearrange("p i j d -> p (i j) d"), in0=both[:, :, 0, :], in1=both[:, :, 1, :], op=ADD)
             heads = out_1[0] if pair == "k" else out_0[0, 2 * pair:2 * pair + 2]
             dst = heads.rearrange("h (p j) d -> p h j d", j=TOK)[:, i0:i1, hh * HALF_TOK:(hh + 1) * HALF_TOK, :]
-            nc.sync.dma_start(out=dst, in_=prod[pair, hh, 0][:, i0:i1].rearrange("p i j f d -> p i j (f d)"))
+            nc.sync.dma_start(out=dst, in_=result[:])
 
         def finish_v(hh):
-            v_out = ring.tile([P, KV, HALF_TOK, D], F32, tag="prod_first", bufs=10, name="v_out")
+            v_out = ring.tile([P, KV, HALF_TOK, D], F32, tag="result", bufs=9, name="v_out")
             for i in range(KV):
                 for j in range(HALF_TOK):
                     tok = hh * HALF_TOK + j
@@ -242,9 +242,7 @@ def tile_multiheadattention_pa_kernel(tc, x, cos, sin, mask, Wq, bq, Wk, bk, Wv,
             load_x(1, c)
             load_w([0, 1], Wq, 0, c)
         for hh in range(2):
-            for axis in range(3):
-                for cs in range(2):
-                    load_table(hh, cs, axis)
+            load_tables(hh)
             load_wq(2 + 2 * hh)
 
         transpose_x(0, 0)
@@ -281,9 +279,10 @@ def tile_multiheadattention_pa_kernel(tc, x, cos, sin, mask, Wq, bq, Wk, bk, Wv,
         interleave_w(1, last, False)
         quantize_w(1, 2, PASSES)
         finish_tables(0, True)
+        mask_tables(nc.gpsimd, 0)
 
         names = list(range(Q_PAIRS - 1)) + ["v", Q_PAIRS - 1]
-        groups = [("k", 0), (0, 0), (1, 0), (2, 0), ("k", 1), (0, 1), (1, 1), (2, 1)]
+        groups = [(0, 0), ("k", 0), (1, 0), (2, 0), (0, 1), ("k", 1), (1, 1), (2, 1)]
         groups += [(pair, hh) for pair in range(3, Q_PAIRS) for hh in range(2)]
 
         project_pair(0, 0)
@@ -293,40 +292,42 @@ def tile_multiheadattention_pa_kernel(tc, x, cos, sin, mask, Wq, bq, Wk, bk, Wv,
         transpose_out(*groups[0])
         project_pair(1, 0)
         transpose_out(*groups[1])
-        interleave_w(3, 0, False)
-        project_pair(0, 1, [None, (2, 1)])
-        interleave_w(2, 2, False)
-        project_pair(1, 1)
         for g in (1, 2):
-            interleave_w(3, g, False)
+            interleave_w(2, g, False)
+        project_pair(0, 1)
+        project_pair(1, 1)
+        interleave_w(3, 0, False)
         rotate(*groups[0])
         interleave_w(2, 0, True)
         add_and_store(nc.gpsimd, *groups[0])
         transpose_out(*groups[2])
-        rotate(*groups[1], steps=ALL_STEPS[:3])
+        rotate(*groups[1], heads=(0,))
         interleave_w(2, 3, True)
+        interleave_w(3, 1, True)
         quantize_w(2, 0, PASSES)
-        rotate(*groups[1], steps=ALL_STEPS[3:])
+        interleave_w(3, 2, True)
+        rotate(*groups[1], heads=(1,))
         add_and_store(nc.gpsimd, *groups[1])
         load_wq(6)
         rotate(*groups[2])
         interleave_w(3, 3, True)
         add_and_store(nc.gpsimd, *groups[2])
         project_pair(2, 0)
+        finish_tables(1, False)
         for i in range(2):
             for g in range(PASSES):
                 project(2, i, 1, g)
-            add_bias(2, i, 1)
             transpose_out(*groups[3 + i])
-        finish_tables(1, False)
-        for g in range(1, PASSES):
+        for g in range(PASSES):
             interleave_w(4, g, False)
+            if g < 2:
+                add_bias(2, g, 1)
         rotate(*groups[3])
         quantize_w(3, 0, PASSES)
         add_and_store(nc.gpsimd, *groups[3])
         transpose_out(*groups[5])
         rotate(*groups[4])
-        interleave_w(4, 0, True)
+        mask_tables(nc.vector, 1)
         add_and_store(nc.gpsimd, *groups[4])
 
         first = names.index(3)

@@ -141,8 +141,8 @@ def tile_multiheadattention_pa_kernel(tc, x, cos, sin, mask, Wq, bq, Wk, bk, Wv,
         def interleave_w(pair, g, on_vector):
             if pair not in w_grouped:
                 w_grouped[pair] = ring.tile([P, PASSES, PAIR, PACK], BF16, tag="w_grouped", bufs=3, align_bytes=64, name="w_grouped")
-            dst = w_grouped[pair][:, g]
-            src = w_raw[pair, g].rearrange("p t n -> p n t")
+            dst = w_grouped[pair][:, g].rearrange("p (c i) t -> p c t i", i=4)
+            src = w_raw[pair, g].rearrange("p t (c i) -> p c t i", i=4)
             if on_vector:
                 nc.vector.tensor_copy(out=dst, in_=src)
             else:

from contextlib import ExitStack

import concourse.mybir as mybir
from concourse.masks import make_identity

S, HIDDEN, H, KV, D = 1024, 2048, 16, 2, 128
SECTIONS = ((0, 16), (16, 40), (40, 64))

FLOPS = 2 * S * HIDDEN * (H + 2 * KV) * D
BYTES = 2 * (S * HIDDEN + 2 * S * D + S + (HIDDEN + 1) * (H + 2 * KV) * D) + 4 * S * (H + 2 * KV) * D

F32 = mybir.dt.float32
BF16 = mybir.dt.bfloat16
U32 = mybir.dt.uint32
U8 = mybir.dt.uint8
E4M3 = mybir.dt.float8_e4m3fn_x4
E5M2 = mybir.dt.float8_e5m2_x4
MULT = mybir.AluOpType.mult
ADD = mybir.AluOpType.add
ACT = mybir.ActivationFunctionType

P = 128
PACK = 4
K_PASS = P * PACK
PASSES = HIDDEN // K_PASS
TOK = S // P
HALF_TOK = TOK // 2
N_HALF = HALF_TOK * P
PAIR = 2 * D
HD = D // 2
Q_PAIRS = H // 2


def tile_multiheadattention_pa_kernel(tc, x, cos, sin, mask, Wq, bq, Wk, bk, Wv, bv, out_0, out_1, out_2):
    nc = tc.nc
    x_tok = x[0].rearrange("(p j) k -> p j k", j=TOK)

    with ExitStack() as ctx:
        keep = ctx.enter_context(tc.tile_pool(name="keep", bufs=1))
        ring = ctx.enter_context(tc.tile_pool(name="ring", bufs=1))
        psum = ctx.enter_context(tc.psum_pool(name="psum", bufs=4))
        ctx.enter_context(tc.manual_schedule())

        ident = keep.tile([P, P], F32)
        ident_bf = keep.tile([P, P], BF16)
        bias_rows = keep.tile([P, D], BF16)
        bias_cols = keep.tile([P, H + 2 * KV], F32)
        mask_bf = keep.tile([P, TOK], BF16)
        mask_f32 = keep.tile([P, TOK], F32)
        rot = keep.tile([P, TOK, 4, HD], BF16)
        rot_last = keep.tile([P, TOK, 4, 32], BF16)
        x_codes = {}
        x_scales = {}
        for hh in range(2):
            for g in range(PASSES):
                x_codes[hh, g] = keep.tile([P, N_HALF], U32, align_bytes=64, name="x_codes_%d_%d" % (hh, g))
                x_scales[hh, g] = keep.tile([P, N_HALF], U8, align_bytes=64, name="x_scales_%d_%d" % (hh, g))

        first_head = {pair: 2 * pair for pair in range(Q_PAIRS)}
        first_head["k"] = H
        first_head["v"] = H + KV
        x_raw, x_grouped, rot_masked = {}, {}, {}
        w_raw, w_grouped, w_codes, w_scales = {}, {}, {}, {}
        acc, chan_major, tok_major, prod = {}, {}, {}, {}

        def load_x(hh, c):
            t = ring.tile([P, HIDDEN], BF16, tag="raw_wide", bufs=12, name="x_raw")
            if hh == 0:
                nc.sync.dma_start(out=t[:].rearrange("p (j k) -> p j k", j=HALF_TOK), in_=x_tok[:, 0:HALF_TOK, c * K_PASS:(c + 1) * K_PASS])
            else:
                nc.sync.dma_start(out=t[:], in_=x_tok[:, HALF_TOK + c, :])
            x_raw[hh, c] = t

        def load_w(pairs, W, col0, g):
            width = PAIR * len(pairs)
            if len(pairs) == 1:
                t = ring.tile([P, PACK, width], BF16, tag="raw_narrow", bufs=4, name="w_narrow")
            else:
                t = ring.tile([P, PACK, width], BF16, tag="raw_wide", bufs=12, name="w_wide")
            rows = W[g * K_PASS:(g + 1) * K_PASS, col0:col0 + width]
            nc.sync.dma_start(out=t[:], in_=rows.rearrange("(p j) n -> p j n", j=PACK))
            for i, pair in enumerate(pairs):
                w_raw[pair, g] = t[:, :, i * PAIR:(i + 1) * PAIR]

        def load_wq(pair):
            for g in range(PASSES):
                load_w([pair, pair + 1], Wq, pair * PAIR, g)

        def load_tables(hh):
            toks = slice(hh * HALF_TOK, (hh + 1) * HALF_TOK)
            order = [(2, slot) for slot in range(4)] + [(axis, slot) for slot in (2, 0, 1, 3) for axis in range(2)]
            for axis, slot in order:
                lo, hi = SECTIONS[axis]
                table, f = ((cos, 0), (sin, 1), (sin, 0), (cos, 1))[slot]
                src = table[axis, 0].rearrange("(p j) (f d) -> p j f d", j=TOK, f=2)[:, toks, f, lo:hi]
                dst = rot[:, toks, slot, lo:hi] if axis < 2 else rot_last[:, toks, slot, 0:hi - lo]
                nc.sync.dma_start(out=dst, in_=src)

        def finish_tables(hh, on_vector):
            lo, hi = SECTIONS[2]
            toks = slice(hh * HALF_TOK, (hh + 1) * HALF_TOK)
            dst = rot[:, toks, :, lo:hi]
            src = rot_last[:, toks, :, 0:hi - lo]
            first_sin = rot[:, toks, 2, :]
            if on_vector:
                nc.vector.tensor_copy(out=dst, in_=src)
                nc.vector.tensor_scalar(out=first_sin, in0=first_sin, scalar1=-1.0, scalar2=None, op0=MULT)
            else:
                nc.scalar.copy(out=dst, in_=src)
                nc.scalar.activation(out=first_sin, in_=first_sin, func=ACT.Copy, scale=-1.0)

        def mask_tables(engine, hh):
            toks = slice(hh * HALF_TOK, (hh + 1) * HALF_TOK)
            t = ring.tile([P, HALF_TOK, 4 * HD], F32, tag="rot_masked", bufs=1, name="rot_masked")
            engine.tensor_tensor(out=t[:], in0=rot[:, toks].rearrange("p j s d -> p j (s d)"),
                                 in1=mask_f32[:, toks].unsqueeze(2).to_broadcast([P, HALF_TOK, 4 * HD]), op=MULT)
            rot_masked[hh] = t

        def transpose_x(hh, g):
            words = x_raw[hh, g][:].bitcast(F32)
            grouped = ring.tile([P, N_HALF * PACK], BF16, tag="x_grouped", bufs=3, align_bytes=64, name="x_grouped")
            x_grouped[hh, g] = grouped
            for b in range(2):
                bank = psum.tile([P, 2, 2, P], F32, tag="turned", name="x_bank")
                for jj in range(2):
                    w0 = (2 * b + jj) * (K_PASS // 2)
                    for u in range(2):
                        nc.tensor.transpose(bank[:, jj, u, :], words[:, w0 + u:w0 + K_PASS // 2:2], ident[:])
                dst = grouped[:, b * 2 * P * PACK:(b + 1) * 2 * P * PACK].bitcast(F32)
                nc.scalar.copy(out=dst.rearrange("p (j r u) -> p j r u", j=2, u=2), in_=bank[:].rearrange("p j u r -> p j r u"))

        def quantize_x(hh, c):
            if hh == 0:
                nc.vector.quantize_mx(out=x_codes[0, c][:].bitcast(E5M2), scales=x_scales[0, c][:], in_=x_grouped[0, c][:])
            else:
                toks = slice(c * P, (c + 1) * P)
                for g in range(PASSES):
                    nc.vector.quantize_mx(out=x_codes[1, g][:, toks].bitcast(E5M2), scales=x_scales[1, g][:, toks],
                                          in_=x_grouped[1, c][:, g * K_PASS:(g + 1) * K_PASS])

        def interleave_w(pair, g, on_vector):
            if pair not in w_grouped:
                w_grouped[pair] = ring.tile([P, PASSES, PAIR, PACK], BF16, tag="w_grouped", bufs=3, align_bytes=64, name="w_grouped")
            dst = w_grouped[pair][:, g].rearrange("p (c i) t -> p c t i", i=4)
            src = w_raw[pair, g].rearrange("p t (c i) -> p c t i", i=4)
            if on_vector:
                nc.vector.tensor_copy(out=dst, in_=src)
            else:
                nc.scalar.copy(out=dst, in_=src)

        def quantize_w(pair, g0, g1):
            if pair not in w_codes:
                w_codes[pair] = ring.tile([P, PASSES, PAIR], U32, tag="w_codes", bufs=4, align_bytes=64, name="w_codes")
                w_scales[pair] = ring.tile([P, PASSES, PAIR], U8, tag="w_scales", bufs=4, align_bytes=64, name="w_scales")
            nc.vector.quantize_mx(out=w_codes[pair][:, g0:g1].rearrange("p g n -> p (g n)").bitcast(E4M3),
                                  scales=w_scales[pair][:, g0:g1].rearrange("p g n -> p (g n)"),
                                  in_=w_grouped[pair][:, g0:g1].rearrange("p g n t -> p (g n t)"))

        def project(pair, i, hh, g):
            if g == 0:
                acc[pair, i, hh] = psum.tile([P, N_HALF], F32, tag="acc", name="acc")
            cols = slice(i * D, (i + 1) * D)
            nc.tensor.matmul_mx(out=acc[pair, i, hh][:], lhsT=w_codes[pair][:, g, cols].bitcast(E4M3), lhsT_scale=w_scales[pair][:, g, cols],
                                rhs=x_codes[hh, g][:].bitcast(E5M2), rhs_scale=x_scales[hh, g][:],
                                start=(g == 0), stop=(g == PASSES - 1))

        def project_keys_second_half(j):
            toks = slice(j * P, (j + 1) * P)
            for i in range(KV):
                if j == 0:
                    acc["k", i, 1] = psum.tile([P, N_HALF], F32, tag="acc", name="acc")
                cols = slice(i * D, (i + 1) * D)
                for g in range(PASSES):
                    nc.tensor.matmul_mx(out=acc["k", i, 1][:, toks], lhsT=w_codes["k"][:, g, cols].bitcast(E4M3), lhsT_scale=w_scales["k"][:, g, cols],
                                        rhs=x_codes[1, g][:, toks].bitcast(E5M2), rhs_scale=x_scales[1, g][:, toks],
                                        start=(g == 0), stop=(g == PASSES - 1))

        def add_bias(pair, i, hh):
            head = first_head[pair] + i
            t = ring.tile([P, N_HALF], F32, tag="chan_major", bufs=10, name="chan_major")
            nc.scalar.activation(out=t[:], in_=acc[pair, i, hh][:], func=ACT.Identity, bias=bias_cols[:, head:head + 1])
            chan_major[pair, i, hh] = t

        def project_pair(pair, hh, scalar_jobs=(None, None)):
            for i in range(2):
                for g in range(PASSES):
                    project(pair, i, hh, g)
                if scalar_jobs[i]:
                    interleave_w(*scalar_jobs[i], False)
                add_bias(pair, i, hh)

        def transpose_out(pair, hh, tag="turned"):
            for b in range(2):
                bank = psum.tile([P, HALF_TOK, D], F32, tag=tag, name="out_bank")
                for s in range(HALF_TOK):
                    nc.tensor.transpose(bank[:, s, :], chan_major[pair, b, hh][:, s * P:(s + 1) * P], ident[:])
                tok_major[pair, b, hh] = bank

        def rotate(pair, hh, heads=(0, 1)):
            if (pair, hh) not in prod:
                prod[pair, hh] = ring.tile([P, 2, HALF_TOK, 2, D], F32, tag="prod", bufs=3, name="prod")
            if pair == "k":
                factors = rot_masked[hh][:].rearrange("p j (f r d) -> p (j f) r d", f=2, r=2)
            else:
                factors = rot[:, hh * HALF_TOK:(hh + 1) * HALF_TOK].rearrange("p j (f r) d -> p (j f) r d", f=2)
            for i in heads:
                halves = tok_major[pair, i, hh][:].rearrange("p j (f d) -> p (j f) d", f=2)
                nc.vector.tensor_tensor(out=prod[pair, hh][:, i].rearrange("p j f (r d) -> p (j f) r d", r=2),
                                        in0=halves.unsqueeze(2).to_broadcast([P, 2 * HALF_TOK, 2, HD]), in1=factors, op=MULT)

        def add_and_store(engine, pair, hh, i0=0, i1=2):
            result = ring.tile([P, i1 - i0, HALF_TOK, D], F32, tag="result", bufs=9, name="result")
            both = prod[pair, hh][:, i0:i1].rearrange("p i j f d -> p (i j) f d")
            engine.tensor_tensor(out=result[:].rearrange("p i j d -> p (i j) d"), in0=both[:, :, 0, :], in1=both[:, :, 1, :], op=ADD)
            heads = out_1[0] if pair == "k" else out_0[0, 2 * pair:2 * pair + 2]
            dst = heads.rearrange("h (p j) d -> p h j d", j=TOK)[:, i0:i1, hh * HALF_TOK:(hh + 1) * HALF_TOK, :]
            nc.sync.dma_start(out=dst, in_=result[:])

        def finish_v(hh):
            v_out = ring.tile([P, KV, HALF_TOK, D], F32, tag="result", bufs=9, name="v_out")
            for i in range(KV):
                for j in range(HALF_TOK):
                    tok = hh * HALF_TOK + j
                    nc.scalar.activation(out=v_out[:, i, j, :], in_=tok_major["v", i, hh][:, j, :], func=ACT.Copy, scale=mask_f32[:, tok:tok + 1])
            nc.sync.dma_start(out=out_2[0].rearrange("h (p j) d -> p h j d", j=TOK)[:, :, hh * HALF_TOK:(hh + 1) * HALF_TOK, :], in_=v_out[:])

        make_identity(nc, ident[:])
        make_identity(nc, ident_bf[:])
        nc.vector.memset(bias_rows[:], 0.0)
        for g in range(2):
            load_x(0, g)
            load_w(["k"], Wk, 0, g)
        nc.scalar.dma_start(out=mask_bf[:], in_=mask[0].rearrange("(p j) -> p j", j=TOK))
        nc.scalar.dma_start(out=bias_rows[0:H, :], in_=bq.rearrange("(h d) -> h d", d=D))
        nc.scalar.dma_start(out=bias_rows[H:H + KV, :], in_=bk.rearrange("(h d) -> h d", d=D))
        nc.scalar.dma_start(out=bias_rows[H + KV:H + 2 * KV, :], in_=bv.rearrange("(h d) -> h d", d=D))
        nc.scalar.activation(out=mask_f32[:], in_=mask_bf[:], func=ACT.Identity)
        for g in range(2, PASSES):
            load_x(0, g)
            load_w(["k"], Wk, 0, g)
        for c in range(PASSES):
            load_x(1, c)
            load_w([0, 1], Wq, 0, c)
        for hh in range(2):
            load_tables(hh)
            load_wq(2 + 2 * hh)

        transpose_x(0, 0)
        bias_bank = psum.tile([P, P], BF16, tag="acc", name="bias_bank")
        nc.tensor.transpose(bias_bank[:], bias_rows[:], ident_bf[:])
        for g in range(PASSES):
            if g + 1 < PASSES:
                transpose_x(0, g + 1)
            else:
                transpose_x(1, 0)
            interleave_w("k", g, True)
            if g == 0:
                nc.vector.tensor_copy(out=bias_cols[:], in_=bias_bank[:, 0:H + 2 * KV])
            quantize_x(0, g)
            quantize_w("k", g, g + 1)
            for i in range(KV):
                project("k", i, 0, g)

        last = PASSES - 1
        for c in range(last):
            if c == 0:
                for i in range(KV):
                    add_bias("k", i, 0)
            interleave_w(0, c, True)
            quantize_x(1, c)
            quantize_w(0, c, c + 1)
            interleave_w(1, c, c == 0)
            transpose_x(1, c + 1)
            project_keys_second_half(c)
        quantize_w(1, 0, 2)
        interleave_w(0, last, True)
        quantize_w(0, last, last + 1)
        quantize_x(1, last)
        interleave_w(1, last, False)
        quantize_w(1, 2, PASSES)
        finish_tables(0, True)
        mask_tables(nc.gpsimd, 0)

        names = list(range(Q_PAIRS - 1)) + ["v", Q_PAIRS - 1]
        groups = [(0, 0), ("k", 0), (1, 0), (2, 0), (0, 1), ("k", 1), (1, 1), (2, 1)]
        groups += [(pair, hh) for pair in range(3, Q_PAIRS) for hh in range(2)]

        project_pair(0, 0)
        project_keys_second_half(last)
        for i in range(KV):
            add_bias("k", i, 1)
        transpose_out(*groups[0])
        project_pair(1, 0)
        transpose_out(*groups[1])
        for g in (1, 2):
            interleave_w(2, g, False)
        project_pair(0, 1)
        project_pair(1, 1)
        interleave_w(3, 0, False)
        rotate(*groups[0])
        interleave_w(2, 0, True)
        add_and_store(nc.gpsimd, *groups[0])
        transpose_out(*groups[2])
        rotate(*groups[1], heads=(0,))
        interleave_w(2, 3, True)
        interleave_w(3, 1, True)
        quantize_w(2, 0, PASSES)
        interleave_w(3, 2, True)
        rotate(*groups[1], heads=(1,))
        add_and_store(nc.gpsimd, *groups[1])
        load_wq(6)
        rotate(*groups[2])
        interleave_w(3, 3, True)
        add_and_store(nc.gpsimd, *groups[2])
        project_pair(2, 0)
        finish_tables(1, False)
        for i in range(2):
            for g in range(PASSES):
                project(2, i, 1, g)
            transpose_out(*groups[3 + i])
        for g in range(PASSES):
            interleave_w(4, g, False)
            if g < 2:
                add_bias(2, g, 1)
        rotate(*groups[3])
        quantize_w(3, 0, PASSES)
        add_and_store(nc.gpsimd, *groups[3])
        transpose_out(*groups[5])
        rotate(*groups[4])
        mask_tables(nc.vector, 1)
        add_and_store(nc.gpsimd, *groups[4])

        first = names.index(3)
        for n in range(2 * (len(names) - first)):
            at, hh = first + n // 2, n % 2
            ahead = names[at + 2] if at + 2 < len(names) else None
            if ahead is None:
                project_pair(names[at], hh)
            elif hh == 0:
                project_pair(names[at], hh, [None, (ahead, 1)])
            else:
                interleave_w(ahead, 2, False)
                project_pair(names[at], hh, [None, (ahead, 3)])
            rotate(*groups[n + 5])
            if hh == 0 and at + 1 < len(names):
                quantize_w(names[at + 1], 0, PASSES)
            elif hh == 1 and ahead is not None:
                interleave_w(ahead, 0, True)
            for v_half in range(2):
                if n == 2 * (names.index("v") - first) + 1 + v_half:
                    transpose_out("v", v_half, tag="acc")
                    finish_v(v_half)
            add_and_store(nc.gpsimd, *groups[n + 5])
            transpose_out(*groups[n + 6])
            if n == 0:
                for g in range(PASSES):
                    load_w(["v"], Wv, 0, g)
        rotate(*groups[-1])
        for i in range(2):
            add_and_store(nc.vector, *groups[-1], i, i + 1)
